import numpy as np
import ml_dtypes

BF16 = ml_dtypes.bfloat16


def bf(x):
    return np.asarray(x, np.float32).astype(BF16)


def f32(x):
    return np.asarray(x, np.float32)


def f64(x):
    return np.asarray(x).astype(np.float64)


def striped(idx):
    return np.tile(idx.reshape(-1, 16).T, (8, 1))


S, D, M, N, NS = 1024, 128, 256, 512, 32


def setup_inputs():
    return {"k_cache": bf(np.random.standard_normal((S, D))), "q": bf(np.random.standard_normal((D, M))), "v": bf(np.random.standard_normal((N, D))), "offs": striped(np.random.permutation(S)[:N])}


def reference(k_cache, q, v, offs):
    idx = offs[:16].T.reshape(-1)
    sc = (f64(q).T @ f64(k_cache)[idx].T) * D ** -0.5
    e = np.exp(sc)
    mx = e.reshape(M, NS, N // NS).sum(axis=2).max(axis=1, keepdims=True)
    return (e / mx) @ f64(v)

@@ -1,0 +1,91 @@
+import concourse.mybir as mybir
+from concourse.masks import make_identity
+
+BF16, F32, U16 = mybir.dt.bfloat16, mybir.dt.float32, mybir.dt.uint16
+EXP = mybir.ActivationFunctionType.Exp
+X = mybir.AxisListType.X
+
+P = 128
+S, D = 1024, 128
+M, N = 256, 512
+SPLIT = 16
+SCALE = D ** -0.5
+S_BLOCKS, M_BLOCKS, N_BLOCKS = S // P, M // P, N // P
+FLOPS = 2 * M * N * D + 2 * M * N * D
+
+
+def tile_spgqaflashdecodeiris_kernel(tc, k_cache, q, v, offs, out):
+    nc = tc.nc
+    with (
+        tc.tile_pool(name="held", bufs=1) as held,
+        tc.tile_pool(name="work", bufs=M_BLOCKS) as work,
+        tc.psum_pool(name="flipped", bufs=2) as flipped,
+        tc.psum_pool(name="scores", bufs=M_BLOCKS) as scores,
+        tc.psum_pool(name="products", bufs=M_BLOCKS) as products,
+    ):
+        k_rows = held.tile([P, S_BLOCKS, D], BF16, name="k_rows")
+        k_blocks = k_cache.rearrange("(b p) d -> p b d", p=P)
+        nc.sync.dma_start(k_rows[:, 0:2, :], k_blocks[:, 0:2, :])
+        nc.scalar.dma_start(k_rows[:, 2:4, :], k_blocks[:, 2:4, :])
+        nc.sync.dma_start(k_rows[:, 4:6, :], k_blocks[:, 4:6, :])
+        nc.scalar.dma_start(k_rows[:, 6:8, :], k_blocks[:, 6:8, :])
+        offsets = held.tile([P, N // 16], U16, name="offsets")
+        nc.sync.dma_start(offsets[:], offs)
+        q_sb = held.tile([D, M], BF16, name="q_sb")
+        nc.sync.dma_start(q_sb[:], q)
+        v_sb = held.tile([P, N_BLOCKS, D], BF16, name="v_sb")
+        nc.scalar.dma_start(v_sb[:], v.rearrange("(b p) f -> p b f", p=P))
+
+        warm = held.tile([P, 1], F32, name="warm")
+        nc.vector.memset(warm[:], 0.0)
+        nc.scalar.activation(warm[:], warm[:], EXP)
+
+        identity = held.tile([P, P], BF16, name="identity")
+        make_identity(nc, identity[:])
+
+        k_t = held.tile([D, S], BF16, name="k_t")
+        for half in range(2):
+            k_flip = flipped.tile([D, 4 * P], BF16, name="k_flip")
+            for b in range(4):
+                nc.tensor.transpose(k_flip[:, b * P:(b + 1) * P], k_rows[:, 4 * half + b, :], identity[:])
+            if half == 0:
+                nc.vector.tensor_copy(k_t[:, 0:4 * P], k_flip[:])
+            else:
+                nc.scalar.copy(k_t[:, 4 * P:8 * P], k_flip[:])
+
+        sc = [scores.tile([P, N], F32, name="sc") for mb in range(M_BLOCKS)]
+        for mb in range(M_BLOCKS):
+            nc.tensor.matmul(sc[mb][:], q_sb[:, mb * P:(mb + 1) * P], k_t[:].indirect(offsets[:]),
+                             start=True, stop=True)
+
+        for mb in range(M_BLOCKS):
+            top = work.tile([P, 1], F32, name="top")
+            nc.vector.reduce_max(top[:], sc[mb][:], axis=X)
+            shift = work.tile([P, 1], F32, name="shift")
+            nc.vector.tensor_scalar_mul(shift[:], top[:], -SCALE)
+            e = work.tile([P, N], F32, name="e")
+            nc.scalar.activation(e[:], sc[mb][:], EXP, bias=shift[:], scale=SCALE)
+            e_bf = work.tile([P, N], BF16, name="e_bf")
+            nc.vector.tensor_copy(e_bf[:], e[:])
+
+            z = work.tile([P, N // SPLIT], F32, name="z")
+            nc.vector.reduce_sum(z[:], e[:].rearrange("m (t s) -> m t s", s=SPLIT), axis=X)
+            mx = work.tile([P, 1], F32, name="mx")
+            nc.vector.reduce_max(mx[:], z[:], axis=X)
+            inv_mx = work.tile([P, 1], F32, name="inv_mx")
+            nc.vector.reciprocal(inv_mx[:], mx[:])
+
+            e_flip = flipped.tile([P, N], BF16, name="e_flip")
+            for jb in range(N_BLOCKS):
+                nc.tensor.transpose(e_flip[:, jb * P:(jb + 1) * P], e_bf[:, jb * P:(jb + 1) * P], identity[:])
+            e_t = work.tile([P, N], BF16, name="e_t")
+            nc.scalar.copy(e_t[:], e_flip[:])
+
+            o_ps = products.tile([P, D], F32, name="o_ps")
+            for jb in range(N_BLOCKS):
+                nc.tensor.matmul(o_ps[:], e_t[:, jb * P:(jb + 1) * P], v_sb[:, jb, :],
+                                 start=(jb == 0), stop=(jb == N_BLOCKS - 1))
+            o_sb = work.tile([P, D], F32, name="o_sb")
+            nc.vector.tensor_scalar_mul(o_sb[:], o_ps[:], inv_mx[:])
+            store = nc.sync if mb == 0 else nc.scalar
+            store.dma_start(out[mb * P:(mb + 1) * P, :], o_sb[:])

@@ -3,6 +3,7 @@ from concourse.masks import make_identity
 
 BF16, F32, U16 = mybir.dt.bfloat16, mybir.dt.float32, mybir.dt.uint16
 EXP = mybir.ActivationFunctionType.Exp
+MAX, MULT = mybir.AluOpType.max, mybir.AluOpType.mult
 X = mybir.AxisListType.X
 
 P = 128
@@ -10,9 +11,11 @@ S, D = 1024, 128
 M, N = 256, 512
 SPLIT = 16
 SCALE = D ** -0.5
-S_BLOCKS, M_BLOCKS, N_BLOCKS = S // P, M // P, N // P
+M_BLOCKS = M // P
+PIECE = 2 * P
 FLOPS = 2 * M * N * D + 2 * M * N * D
-
+PIECES = N // PIECE
+UNITS = M_BLOCKS * PIECES
 
 def tile_spgqaflashdecodeiris_kernel(tc, k_cache, q, v, offs, out):
     nc = tc.nc
@@ -20,10 +23,10 @@ def tile_spgqaflashdecodeiris_kernel(tc, k_cache, q, v, offs, out):
         tc.tile_pool(name="held", bufs=1) as held,
         tc.tile_pool(name="work", bufs=M_BLOCKS) as work,
         tc.psum_pool(name="flipped", bufs=2) as flipped,
-        tc.psum_pool(name="scores", bufs=M_BLOCKS) as scores,
+        tc.psum_pool(name="scores", bufs=UNITS) as scores,
         tc.psum_pool(name="products", bufs=M_BLOCKS) as products,
     ):
-        k_rows = held.tile([P, S_BLOCKS, D], BF16, name="k_rows")
+        k_rows = held.tile([P, S // P, D], BF16, name="k_rows")
         k_blocks = k_cache.rearrange("(b p) d -> p b d", p=P)
         nc.sync.dma_start(k_rows[:, 0:2, :], k_blocks[:, 0:2, :])
         nc.scalar.dma_start(k_rows[:, 2:4, :], k_blocks[:, 2:4, :])
@@ -33,8 +36,6 @@ def tile_spgqaflashdecodeiris_kernel(tc, k_cache, q, v, offs, out):
         nc.sync.dma_start(offsets[:], offs)
         q_sb = held.tile([D, M], BF16, name="q_sb")
         nc.sync.dma_start(q_sb[:], q)
-        v_sb = held.tile([P, N_BLOCKS, D], BF16, name="v_sb")
-        nc.scalar.dma_start(v_sb[:], v.rearrange("(b p) f -> p b f", p=P))
 
         warm = held.tile([P, 1], F32, name="warm")
         nc.vector.memset(warm[:], 0.0)
@@ -42,50 +43,78 @@ def tile_spgqaflashdecodeiris_kernel(tc, k_cache, q, v, offs, out):
 
         identity = held.tile([P, P], BF16, name="identity")
         make_identity(nc, identity[:])
+        v_sb = held.tile([P, N // P, D], BF16, name="v_sb")
+        nc.gpsimd.dma_start(v_sb[:], v.rearrange("(b p) f -> p b f", p=P))
 
         k_t = held.tile([D, S], BF16, name="k_t")
-        for half in range(2):
-            k_flip = flipped.tile([D, 4 * P], BF16, name="k_flip")
-            for b in range(4):
-                nc.tensor.transpose(k_flip[:, b * P:(b + 1) * P], k_rows[:, 4 * half + b, :], identity[:])
-            if half == 0:
-                nc.vector.tensor_copy(k_t[:, 0:4 * P], k_flip[:])
+        for c in range(S // PIECE):
+            k_flip = flipped.tile([D, PIECE], BF16, name="k_flip", tag="flip")
+            for b in range(2):
+                nc.tensor.transpose(k_flip[:, b * P:(b + 1) * P], k_rows[:, 2 * c + b, :], identity[:])
+            if c % 2 == 0:
+                nc.vector.tensor_copy(k_t[:, c * PIECE:(c + 1) * PIECE], k_flip[:])
             else:
-                nc.scalar.copy(k_t[:, 4 * P:8 * P], k_flip[:])
+                nc.scalar.copy(k_t[:, c * PIECE:(c + 1) * PIECE], k_flip[:])
 
-        sc = [scores.tile([P, N], F32, name="sc") for mb in range(M_BLOCKS)]
-        for mb in range(M_BLOCKS):
-            nc.tensor.matmul(sc[mb][:], q_sb[:, mb * P:(mb + 1) * P], k_t[:].indirect(offsets[:]),
+        sc = [scores.tile([P, PIECE], F32, name="sc") for u in range(UNITS)]
+        for u in range(UNITS):
+            mb, c = divmod(u, PIECES)
+            nc.tensor.matmul(sc[u][:], q_sb[:, mb * P:(mb + 1) * P],
+                             k_t[:].indirect(offsets[:, c * (PIECE // 16):(c + 1) * (PIECE // 16)]),
                              start=True, stop=True)
 
+        shift = [work.tile([P, 1], F32, name="shift") for mb in range(M_BLOCKS)]
         for mb in range(M_BLOCKS):
-            top = work.tile([P, 1], F32, name="top")
-            nc.vector.reduce_max(top[:], sc[mb][:], axis=X)
-            shift = work.tile([P, 1], F32, name="shift")
-            nc.vector.tensor_scalar_mul(shift[:], top[:], -SCALE)
-            e = work.tile([P, N], F32, name="e")
-            nc.scalar.activation(e[:], sc[mb][:], EXP, bias=shift[:], scale=SCALE)
-            e_bf = work.tile([P, N], BF16, name="e_bf")
-            nc.vector.tensor_copy(e_bf[:], e[:])
+            top = work.tile([P, PIECES], F32, name="top")
+            for c in range(PIECES):
+                nc.vector.reduce_max(top[:, c:c + 1], sc[mb * PIECES + c][:], axis=X)
+            nc.vector.tensor_scalar(shift[mb][:], top[:, 0:1], top[:, 1:2], -SCALE, op0=MAX, op1=MULT)
 
+        e = [work.tile([P, N], F32, name="e") for mb in range(M_BLOCKS)]
+        e_bf = [work.tile([P, N], BF16, name="e_bf") for mb in range(M_BLOCKS)]
+        e_t = [work.tile([P, N], BF16, name="e_t") for mb in range(M_BLOCKS)]
+        o_ps = [products.tile([P, D], F32, name="o_ps") for mb in range(M_BLOCKS)]
+
+        def exponentiate(u):
+            mb, c = divmod(u, PIECES)
+            piece = slice(c * PIECE, (c + 1) * PIECE)
+            nc.scalar.activation(e[mb][:, piece], sc[u][:], EXP, bias=shift[mb][:], scale=SCALE)
+            nc.vector.tensor_copy(e_bf[mb][:, piece], e[mb][:, piece])
+
+        def flip(u):
+            mb, c = divmod(u, PIECES)
+            e_flip = flipped.tile([P, PIECE], BF16, name="e_flip", tag="flip")
+            for b in range(2):
+                jb = 2 * c + b
+                nc.tensor.transpose(e_flip[:, b * P:(b + 1) * P], e_bf[mb][:, jb * P:(jb + 1) * P], identity[:])
+            if mb == 0:
+                nc.vector.tensor_copy(e_t[mb][:, c * PIECE:(c + 1) * PIECE], e_flip[:])
+            else:
+                nc.scalar.copy(e_t[mb][:, c * PIECE:(c + 1) * PIECE], e_flip[:])
+
+        def multiply(u):
+            mb, c = divmod(u, PIECES)
+            for b in range(2):
+                jb = 2 * c + b
+                nc.tensor.matmul(o_ps[mb][:], e_t[mb][:, jb * P:(jb + 1) * P], v_sb[:, jb, :],
+                                 start=(jb == 0), stop=(jb == N // P - 1))
+
+        for step in range(UNITS + 2):
+            if step < UNITS:
+                exponentiate(step)
+            if 1 <= step <= UNITS:
+                flip(step - 1)
+            if step >= 2:
+                multiply(step - 2)
+
+        for mb in range(M_BLOCKS):
             z = work.tile([P, N // SPLIT], F32, name="z")
-            nc.vector.reduce_sum(z[:], e[:].rearrange("m (t s) -> m t s", s=SPLIT), axis=X)
+            nc.vector.reduce_sum(z[:], e[mb][:].rearrange("m (t s) -> m t s", s=SPLIT), axis=X)
             mx = work.tile([P, 1], F32, name="mx")
             nc.vector.reduce_max(mx[:], z[:], axis=X)
             inv_mx = work.tile([P, 1], F32, name="inv_mx")
             nc.vector.reciprocal(inv_mx[:], mx[:])
-
-            e_flip = flipped.tile([P, N], BF16, name="e_flip")
-            for jb in range(N_BLOCKS):
-                nc.tensor.transpose(e_flip[:, jb * P:(jb + 1) * P], e_bf[:, jb * P:(jb + 1) * P], identity[:])
-            e_t = work.tile([P, N], BF16, name="e_t")
-            nc.scalar.copy(e_t[:], e_flip[:])
-
-            o_ps = products.tile([P, D], F32, name="o_ps")
-            for jb in range(N_BLOCKS):
-                nc.tensor.matmul(o_ps[:], e_t[:, jb * P:(jb + 1) * P], v_sb[:, jb, :],
-                                 start=(jb == 0), stop=(jb == N_BLOCKS - 1))
             o_sb = work.tile([P, D], F32, name="o_sb")
-            nc.vector.tensor_scalar_mul(o_sb[:], o_ps[:], inv_mx[:])
+            nc.vector.tensor_scalar_mul(o_sb[:], o_ps[mb][:], inv_mx[:])
             store = nc.sync if mb == 0 else nc.scalar
             store.dma_start(out[mb * P:(mb + 1) * P, :], o_sb[:])

@@ -16,6 +16,7 @@ PIECE = 2 * P
 FLOPS = 2 * M * N * D + 2 * M * N * D
 PIECES = N // PIECE
 UNITS = M_BLOCKS * PIECES
+WARM_UP_MATMULS = 4
 
 def tile_spgqaflashdecodeiris_kernel(tc, k_cache, q, v, offs, out):
     nc = tc.nc
@@ -36,6 +37,12 @@ def tile_spgqaflashdecodeiris_kernel(tc, k_cache, q, v, offs, out):
         nc.sync.dma_start(offsets[:], offs)
         q_sb = held.tile([D, M], BF16, name="q_sb")
         nc.sync.dma_start(q_sb[:], q)
+
+        zeros = held.tile([P, 4 * P], BF16, name="zeros")
+        nc.gpsimd.memset(zeros[:], 0.0)
+        idle_product = flipped.tile([P, 4 * P], BF16, name="idle_product", tag="flip")
+        for i in range(WARM_UP_MATMULS):
+            nc.tensor.matmul(idle_product[:], zeros[:, 0:P], zeros[:], start=True, stop=True)
 
         warm = held.tile([P, 1], F32, name="warm")
         nc.vector.memset(warm[:], 0.0)

@@ -3,7 +3,6 @@ from concourse.masks import make_identity
 
 BF16, F32, U16 = mybir.dt.bfloat16, mybir.dt.float32, mybir.dt.uint16
 EXP = mybir.ActivationFunctionType.Exp
-MAX, MULT = mybir.AluOpType.max, mybir.AluOpType.mult
 X = mybir.AxisListType.X
 
 P = 128
@@ -12,11 +11,11 @@ M, N = 256, 512
 SPLIT = 16
 SCALE = D ** -0.5
 M_BLOCKS = M // P
-PIECE = 2 * P
+N_BLOCKS = N // P
 FLOPS = 2 * M * N * D + 2 * M * N * D
-PIECES = N // PIECE
-UNITS = M_BLOCKS * PIECES
 WARM_UP_MATMULS = 4
+FILLER_MATMULS = 3
+
 
 def tile_spgqaflashdecodeiris_kernel(tc, k_cache, q, v, offs, out):
     nc = tc.nc
@@ -24,7 +23,7 @@ def tile_spgqaflashdecodeiris_kernel(tc, k_cache, q, v, offs, out):
         tc.tile_pool(name="held", bufs=1) as held,
         tc.tile_pool(name="work", bufs=M_BLOCKS) as work,
         tc.psum_pool(name="flipped", bufs=2) as flipped,
-        tc.psum_pool(name="scores", bufs=UNITS) as scores,
+        tc.psum_pool(name="scores", bufs=M_BLOCKS) as scores,
         tc.psum_pool(name="products", bufs=M_BLOCKS) as products,
     ):
         k_rows = held.tile([P, S // P, D], BF16, name="k_rows")
@@ -37,12 +36,18 @@ def tile_spgqaflashdecodeiris_kernel(tc, k_cache, q, v, offs, out):
         nc.sync.dma_start(offsets[:], offs)
         q_sb = held.tile([D, M], BF16, name="q_sb")
         nc.sync.dma_start(q_sb[:], q)
+        v_sb = held.tile([P, N_BLOCKS, D], BF16, name="v_sb")
+        nc.scalar.dma_start(v_sb[:], v.rearrange("(b p) f -> p b f", p=P))
 
         zeros = held.tile([P, 4 * P], BF16, name="zeros")
         nc.gpsimd.memset(zeros[:], 0.0)
-        idle_product = flipped.tile([P, 4 * P], BF16, name="idle_product", tag="flip")
-        for i in range(WARM_UP_MATMULS):
-            nc.tensor.matmul(idle_product[:], zeros[:, 0:P], zeros[:], start=True, stop=True)
+
+        def keep_tensor_engine_busy(matmuls):
+            idle_product = flipped.tile([P, 4 * P], BF16, name="idle_product", tag="k_flip")
+            for i in range(matmuls):
+                nc.tensor.matmul(idle_product[:], zeros[:, 0:P], zeros[:], start=True, stop=True)
+
+        keep_tensor_engine_busy(WARM_UP_MATMULS)
 
         warm = held.tile([P, 1], F32, name="warm")
         nc.vector.memset(warm[:], 0.0)
@@ -50,78 +55,51 @@ def tile_spgqaflashdecodeiris_kernel(tc, k_cache, q, v, offs, out):
 
         identity = held.tile([P, P], BF16, name="identity")
         make_identity(nc, identity[:])
-        v_sb = held.tile([P, N // P, D], BF16, name="v_sb")
-        nc.gpsimd.dma_start(v_sb[:], v.rearrange("(b p) f -> p b f", p=P))
 
         k_t = held.tile([D, S], BF16, name="k_t")
-        for c in range(S // PIECE):
-            k_flip = flipped.tile([D, PIECE], BF16, name="k_flip", tag="flip")
-            for b in range(2):
-                nc.tensor.transpose(k_flip[:, b * P:(b + 1) * P], k_rows[:, 2 * c + b, :], identity[:])
-            if c % 2 == 0:
-                nc.vector.tensor_copy(k_t[:, c * PIECE:(c + 1) * PIECE], k_flip[:])
+        for half in range(2):
+            k_flip = flipped.tile([D, 4 * P], BF16, name="k_flip")
+            for b in range(4):
+                nc.tensor.transpose(k_flip[:, b * P:(b + 1) * P], k_rows[:, 4 * half + b, :], identity[:])
+            if half == 0:
+                nc.vector.tensor_copy(k_t[:, 0:4 * P], k_flip[:])
             else:
-                nc.scalar.copy(k_t[:, c * PIECE:(c + 1) * PIECE], k_flip[:])
+                nc.scalar.copy(k_t[:, 4 * P:8 * P], k_flip[:])
 
-        sc = [scores.tile([P, PIECE], F32, name="sc") for u in range(UNITS)]
-        for u in range(UNITS):
-            mb, c = divmod(u, PIECES)
-            nc.tensor.matmul(sc[u][:], q_sb[:, mb * P:(mb + 1) * P],
-                             k_t[:].indirect(offsets[:, c * (PIECE // 16):(c + 1) * (PIECE // 16)]),
+        sc = [scores.tile([P, N], F32, name="sc") for mb in range(M_BLOCKS)]
+        for mb in range(M_BLOCKS):
+            nc.tensor.matmul(sc[mb][:], q_sb[:, mb * P:(mb + 1) * P], k_t[:].indirect(offsets[:]),
                              start=True, stop=True)
-
-        shift = [work.tile([P, 1], F32, name="shift") for mb in range(M_BLOCKS)]
-        for mb in range(M_BLOCKS):
-            top = work.tile([P, PIECES], F32, name="top")
-            for c in range(PIECES):
-                nc.vector.reduce_max(top[:, c:c + 1], sc[mb * PIECES + c][:], axis=X)
-            nc.vector.tensor_scalar(shift[mb][:], top[:, 0:1], top[:, 1:2], -SCALE, op0=MAX, op1=MULT)
-
-        e = [work.tile([P, N], F32, name="e") for mb in range(M_BLOCKS)]
-        e_bf = [work.tile([P, N], BF16, name="e_bf") for mb in range(M_BLOCKS)]
-        e_t = [work.tile([P, N], BF16, name="e_t") for mb in range(M_BLOCKS)]
-        o_ps = [products.tile([P, D], F32, name="o_ps") for mb in range(M_BLOCKS)]
-
-        def exponentiate(u):
-            mb, c = divmod(u, PIECES)
-            piece = slice(c * PIECE, (c + 1) * PIECE)
-            nc.scalar.activation(e[mb][:, piece], sc[u][:], EXP, bias=shift[mb][:], scale=SCALE)
-            nc.vector.tensor_copy(e_bf[mb][:, piece], e[mb][:, piece])
-
-        def flip(u):
-            mb, c = divmod(u, PIECES)
-            e_flip = flipped.tile([P, PIECE], BF16, name="e_flip", tag="flip")
-            for b in range(2):
-                jb = 2 * c + b
-                nc.tensor.transpose(e_flip[:, b * P:(b + 1) * P], e_bf[mb][:, jb * P:(jb + 1) * P], identity[:])
-            if mb == 0:
-                nc.vector.tensor_copy(e_t[mb][:, c * PIECE:(c + 1) * PIECE], e_flip[:])
-            else:
-                nc.scalar.copy(e_t[mb][:, c * PIECE:(c + 1) * PIECE], e_flip[:])
-
-        def multiply(u):
-            mb, c = divmod(u, PIECES)
-            for b in range(2):
-                jb = 2 * c + b
-                nc.tensor.matmul(o_ps[mb][:], e_t[mb][:, jb * P:(jb + 1) * P], v_sb[:, jb, :],
-                                 start=(jb == 0), stop=(jb == N // P - 1))
-
-        for step in range(UNITS + 2):
-            if step < UNITS:
-                exponentiate(step)
-            if 1 <= step <= UNITS:
-                flip(step - 1)
-            if step >= 2:
-                multiply(step - 2)
+        keep_tensor_engine_busy(FILLER_MATMULS)
 
         for mb in range(M_BLOCKS):
+            top = work.tile([P, 1], F32, name="top")
+            nc.vector.reduce_max(top[:], sc[mb][:], axis=X)
+            shift = work.tile([P, 1], F32, name="shift")
+            nc.vector.tensor_scalar_mul(shift[:], top[:], -SCALE)
+            e = work.tile([P, N], F32, name="e")
+            nc.scalar.activation(e[:], sc[mb][:], EXP, bias=shift[:], scale=SCALE)
+            e_bf = work.tile([P, N], BF16, name="e_bf")
+            nc.vector.tensor_copy(e_bf[:], e[:])
+
             z = work.tile([P, N // SPLIT], F32, name="z")
-            nc.vector.reduce_sum(z[:], e[mb][:].rearrange("m (t s) -> m t s", s=SPLIT), axis=X)
+            nc.vector.reduce_sum(z[:], e[:].rearrange("m (t s) -> m t s", s=SPLIT), axis=X)
             mx = work.tile([P, 1], F32, name="mx")
             nc.vector.reduce_max(mx[:], z[:], axis=X)
             inv_mx = work.tile([P, 1], F32, name="inv_mx")
             nc.vector.reciprocal(inv_mx[:], mx[:])
+
+            e_flip = flipped.tile([P, N], BF16, name="e_flip")
+            for jb in range(N_BLOCKS):
+                nc.tensor.transpose(e_flip[:, jb * P:(jb + 1) * P], e_bf[:, jb * P:(jb + 1) * P], identity[:])
+            e_t = work.tile([P, N], BF16, name="e_t")
+            nc.scalar.copy(e_t[:], e_flip[:])
+
+            o_ps = products.tile([P, D], F32, name="o_ps")
+            for jb in range(N_BLOCKS):
+                nc.tensor.matmul(o_ps[:], e_t[:, jb * P:(jb + 1) * P], v_sb[:, jb, :],
+                                 start=(jb == 0), stop=(jb == N_BLOCKS - 1))
             o_sb = work.tile([P, D], F32, name="o_sb")
-            nc.vector.tensor_scalar_mul(o_sb[:], o_ps[mb][:], inv_mx[:])
+            nc.vector.tensor_scalar_mul(o_sb[:], o_ps[:], inv_mx[:])
             store = nc.sync if mb == 0 else nc.scalar
             store.dma_start(out[mb * P:(mb + 1) * P, :], o_sb[:])

@@ -13,8 +13,7 @@ SCALE = D ** -0.5
 M_BLOCKS = M // P
 N_BLOCKS = N // P
 FLOPS = 2 * M * N * D + 2 * M * N * D
-WARM_UP_MATMULS = 4
-FILLER_MATMULS = 3
+FILLER_MATMULS = 2
 
 
 def tile_spgqaflashdecodeiris_kernel(tc, k_cache, q, v, offs, out):
@@ -39,15 +38,8 @@ def tile_spgqaflashdecodeiris_kernel(tc, k_cache, q, v, offs, out):
         v_sb = held.tile([P, N_BLOCKS, D], BF16, name="v_sb")
         nc.scalar.dma_start(v_sb[:], v.rearrange("(b p) f -> p b f", p=P))
 
-        zeros = held.tile([P, 4 * P], BF16, name="zeros")
+        zeros = held.tile([P, P], BF16, name="zeros")
         nc.gpsimd.memset(zeros[:], 0.0)
-
-        def keep_tensor_engine_busy(matmuls):
-            idle_product = flipped.tile([P, 4 * P], BF16, name="idle_product", tag="k_flip")
-            for i in range(matmuls):
-                nc.tensor.matmul(idle_product[:], zeros[:, 0:P], zeros[:], start=True, stop=True)
-
-        keep_tensor_engine_busy(WARM_UP_MATMULS)
 
         warm = held.tile([P, 1], F32, name="warm")
         nc.vector.memset(warm[:], 0.0)
@@ -70,7 +62,10 @@ def tile_spgqaflashdecodeiris_kernel(tc, k_cache, q, v, offs, out):
         for mb in range(M_BLOCKS):
             nc.tensor.matmul(sc[mb][:], q_sb[:, mb * P:(mb + 1) * P], k_t[:].indirect(offsets[:]),
                              start=True, stop=True)
-        keep_tensor_engine_busy(FILLER_MATMULS)
+
+        idle_product = flipped.tile([P, 4 * P], BF16, name="idle_product", tag="k_flip")
+        for i in range(FILLER_MATMULS):
+            nc.tensor.matmul(idle_product[:], zeros[:], k_t[:, 0:4 * P], start=True, stop=True)
 
         for mb in range(M_BLOCKS):
             top = work.tile([P, 1], F32, name="top")
@@ -91,7 +86,8 @@ def tile_spgqaflashdecodeiris_kernel(tc, k_cache, q, v, offs, out):
 
             e_flip = flipped.tile([P, N], BF16, name="e_flip")
             for jb in range(N_BLOCKS):
-                nc.tensor.transpose(e_flip[:, jb * P:(jb + 1) * P], e_bf[:, jb * P:(jb + 1) * P], identity[:])
+                nc.tensor.matmul(e_flip[:, jb * P:(jb + 1) * P], e_bf[:, jb * P:(jb + 1) * P], identity[:],
+                                 start=True, stop=True)
             e_t = work.tile([P, N], BF16, name="e_t")
             nc.scalar.copy(e_t[:], e_flip[:])
 

@@ -13,7 +13,7 @@ SCALE = D ** -0.5
 M_BLOCKS = M // P
 N_BLOCKS = N // P
 FLOPS = 2 * M * N * D + 2 * M * N * D
-FILLER_MATMULS = 2
+WARM_UP_MATMULS = 4
 
 
 def tile_spgqaflashdecodeiris_kernel(tc, k_cache, q, v, offs, out):
@@ -38,8 +38,11 @@ def tile_spgqaflashdecodeiris_kernel(tc, k_cache, q, v, offs, out):
         v_sb = held.tile([P, N_BLOCKS, D], BF16, name="v_sb")
         nc.scalar.dma_start(v_sb[:], v.rearrange("(b p) f -> p b f", p=P))
 
-        zeros = held.tile([P, P], BF16, name="zeros")
+        zeros = held.tile([P, 4 * P], BF16, name="zeros")
         nc.gpsimd.memset(zeros[:], 0.0)
+        idle_product = flipped.tile([P, 4 * P], BF16, name="idle_product", tag="k_flip")
+        for i in range(WARM_UP_MATMULS):
+            nc.tensor.matmul(idle_product[:], zeros[:, 0:P], zeros[:], start=True, stop=True)
 
         warm = held.tile([P, 1], F32, name="warm")
         nc.vector.memset(warm[:], 0.0)
@@ -63,39 +66,40 @@ def tile_spgqaflashdecodeiris_kernel(tc, k_cache, q, v, offs, out):
             nc.tensor.matmul(sc[mb][:], q_sb[:, mb * P:(mb + 1) * P], k_t[:].indirect(offsets[:]),
                              start=True, stop=True)
 
-        idle_product = flipped.tile([P, 4 * P], BF16, name="idle_product", tag="k_flip")
-        for i in range(FILLER_MATMULS):
-            nc.tensor.matmul(idle_product[:], zeros[:], k_t[:, 0:4 * P], start=True, stop=True)
-
+        shift = [work.tile([P, 1], F32, name="shift") for mb in range(M_BLOCKS)]
+        e_bf = [work.tile([P, N], BF16, name="e_bf") for mb in range(M_BLOCKS)]
         for mb in range(M_BLOCKS):
             top = work.tile([P, 1], F32, name="top")
             nc.vector.reduce_max(top[:], sc[mb][:], axis=X)
-            shift = work.tile([P, 1], F32, name="shift")
-            nc.vector.tensor_scalar_mul(shift[:], top[:], -SCALE)
-            e = work.tile([P, N], F32, name="e")
-            nc.scalar.activation(e[:], sc[mb][:], EXP, bias=shift[:], scale=SCALE)
-            e_bf = work.tile([P, N], BF16, name="e_bf")
-            nc.vector.tensor_copy(e_bf[:], e[:])
+            nc.vector.tensor_scalar_mul(shift[mb][:], top[:], -SCALE)
+            nc.scalar.activation(e_bf[mb][:], sc[mb][:], EXP, bias=shift[mb][:], scale=SCALE)
 
-            z = work.tile([P, N // SPLIT], F32, name="z")
-            nc.vector.reduce_sum(z[:], e[:].rearrange("m (t s) -> m t s", s=SPLIT), axis=X)
-            mx = work.tile([P, 1], F32, name="mx")
-            nc.vector.reduce_max(mx[:], z[:], axis=X)
-            inv_mx = work.tile([P, 1], F32, name="inv_mx")
-            nc.vector.reciprocal(inv_mx[:], mx[:])
-
+        o_ps = [products.tile([P, D], F32, name="o_ps") for mb in range(M_BLOCKS)]
+        for mb in range(M_BLOCKS):
             e_flip = flipped.tile([P, N], BF16, name="e_flip")
             for jb in range(N_BLOCKS):
-                nc.tensor.matmul(e_flip[:, jb * P:(jb + 1) * P], e_bf[:, jb * P:(jb + 1) * P], identity[:],
-                                 start=True, stop=True)
+                nc.tensor.transpose(e_flip[:, jb * P:(jb + 1) * P], e_bf[mb][:, jb * P:(jb + 1) * P], identity[:])
             e_t = work.tile([P, N], BF16, name="e_t")
-            nc.scalar.copy(e_t[:], e_flip[:])
-
-            o_ps = products.tile([P, D], F32, name="o_ps")
+            if mb == 0:
+                nc.vector.tensor_copy(e_t[:], e_flip[:])
+            else:
+                nc.scalar.copy(e_t[:], e_flip[:])
             for jb in range(N_BLOCKS):
-                nc.tensor.matmul(o_ps[:], e_t[:, jb * P:(jb + 1) * P], v_sb[:, jb, :],
+                nc.tensor.matmul(o_ps[mb][:], e_t[:, jb * P:(jb + 1) * P], v_sb[:, jb, :],
                                  start=(jb == 0), stop=(jb == N_BLOCKS - 1))
-            o_sb = work.tile([P, D], F32, name="o_sb")
-            nc.vector.tensor_scalar_mul(o_sb[:], o_ps[:], inv_mx[:])
-            store = nc.sync if mb == 0 else nc.scalar
-            store.dma_start(out[mb * P:(mb + 1) * P, :], o_sb[:])
+
+        z = held.tile([P, M_BLOCKS, N // SPLIT], F32, name="z")
+        for mb in range(M_BLOCKS):
+            e = work.tile([P, N], F32, name="e")
+            nc.scalar.activation(e[:], sc[mb][:], EXP, bias=shift[mb][:], scale=SCALE)
+            nc.vector.reduce_sum(z[:, mb, :], e[:].rearrange("m (t s) -> m t s", s=SPLIT), axis=X)
+        mx = held.tile([P, M_BLOCKS], F32, name="mx")
+        nc.vector.reduce_max(mx[:], z[:], axis=X)
+        inv_mx = held.tile([P, M_BLOCKS], F32, name="inv_mx")
+        nc.vector.reciprocal(inv_mx[:], mx[:])
+
+        o_sb = [work.tile([P, D], F32, name="o_sb") for mb in range(M_BLOCKS)]
+        nc.scalar.mul(o_sb[0][:], o_ps[0][:], inv_mx[:, 0:1])
+        nc.vector.tensor_scalar_mul(o_sb[1][:], o_ps[1][:], inv_mx[:, 1:2])
+        nc.scalar.dma_start(out[0:P, :], o_sb[0][:])
+        nc.sync.dma_start(out[P:2 * P, :], o_sb[1][:])

@@ -13,7 +13,6 @@ SCALE = D ** -0.5
 M_BLOCKS = M // P
 N_BLOCKS = N // P
 FLOPS = 2 * M * N * D + 2 * M * N * D
-WARM_UP_MATMULS = 4
 
 
 def tile_spgqaflashdecodeiris_kernel(tc, k_cache, q, v, offs, out):
@@ -37,12 +36,6 @@ def tile_spgqaflashdecodeiris_kernel(tc, k_cache, q, v, offs, out):
         nc.sync.dma_start(q_sb[:], q)
         v_sb = held.tile([P, N_BLOCKS, D], BF16, name="v_sb")
         nc.scalar.dma_start(v_sb[:], v.rearrange("(b p) f -> p b f", p=P))
-
-        zeros = held.tile([P, 4 * P], BF16, name="zeros")
-        nc.gpsimd.memset(zeros[:], 0.0)
-        idle_product = flipped.tile([P, 4 * P], BF16, name="idle_product", tag="k_flip")
-        for i in range(WARM_UP_MATMULS):
-            nc.tensor.matmul(idle_product[:], zeros[:, 0:P], zeros[:], start=True, stop=True)
 
         warm = held.tile([P, 1], F32, name="warm")
         nc.vector.memset(warm[:], 0.0)

@@ -3,6 +3,7 @@ from concourse.masks import make_identity
 
 BF16, F32, U16 = mybir.dt.bfloat16, mybir.dt.float32, mybir.dt.uint16
 EXP = mybir.ActivationFunctionType.Exp
+MULT, MIN = mybir.AluOpType.mult, mybir.AluOpType.min
 X = mybir.AxisListType.X
 
 P = 128
@@ -10,8 +11,7 @@ S, D = 1024, 128
 M, N = 256, 512
 SPLIT = 16
 SCALE = D ** -0.5
-M_BLOCKS = M // P
-N_BLOCKS = N // P
+S_BLOCKS, M_BLOCKS, N_BLOCKS = S // P, M // P, N // P
 FLOPS = 2 * M * N * D + 2 * M * N * D
 
 
@@ -24,7 +24,7 @@ def tile_spgqaflashdecodeiris_kernel(tc, k_cache, q, v, offs, out):
         tc.psum_pool(name="scores", bufs=M_BLOCKS) as scores,
         tc.psum_pool(name="products", bufs=M_BLOCKS) as products,
     ):
-        k_rows = held.tile([P, S // P, D], BF16, name="k_rows")
+        k_rows = held.tile([P, S_BLOCKS, D], BF16, name="k_rows")
         k_blocks = k_cache.rearrange("(b p) d -> p b d", p=P)
         nc.sync.dma_start(k_rows[:, 0:2, :], k_blocks[:, 0:2, :])
         nc.scalar.dma_start(k_rows[:, 2:4, :], k_blocks[:, 2:4, :])
@@ -59,40 +59,33 @@ def tile_spgqaflashdecodeiris_kernel(tc, k_cache, q, v, offs, out):
             nc.tensor.matmul(sc[mb][:], q_sb[:, mb * P:(mb + 1) * P], k_t[:].indirect(offsets[:]),
                              start=True, stop=True)
 
-        shift = [work.tile([P, 1], F32, name="shift") for mb in range(M_BLOCKS)]
-        e_bf = [work.tile([P, N], BF16, name="e_bf") for mb in range(M_BLOCKS)]
         for mb in range(M_BLOCKS):
-            top = work.tile([P, 1], F32, name="top")
-            nc.vector.reduce_max(top[:], sc[mb][:], axis=X)
-            nc.vector.tensor_scalar_mul(shift[mb][:], top[:], -SCALE)
-            nc.scalar.activation(e_bf[mb][:], sc[mb][:], EXP, bias=shift[mb][:], scale=SCALE)
+            scaled = work.tile([P, N], BF16, name="scaled")
+            shift = work.tile([P, 1], F32, name="shift")
+            nc.vector.tensor_scalar(scaled[:], sc[mb][:], -SCALE, None, op0=MULT, op1=MIN, accum_out=shift[:])
+            e = work.tile([P, N], F32, name="e")
+            nc.scalar.activation(e[:], sc[mb][:], EXP, bias=shift[:], scale=SCALE)
+            e_bf = work.tile([P, N], BF16, name="e_bf")
+            nc.vector.tensor_copy(e_bf[:], e[:])
 
-        o_ps = [products.tile([P, D], F32, name="o_ps") for mb in range(M_BLOCKS)]
-        for mb in range(M_BLOCKS):
+            z = work.tile([P, N // SPLIT], F32, name="z")
+            nc.vector.reduce_sum(z[:], e[:].rearrange("m (t s) -> m t s", s=SPLIT), axis=X)
+            mx = work.tile([P, 1], F32, name="mx")
+            nc.vector.reduce_max(mx[:], z[:], axis=X)
+            inv_mx = work.tile([P, 1], F32, name="inv_mx")
+            nc.vector.reciprocal(inv_mx[:], mx[:])
+
             e_flip = flipped.tile([P, N], BF16, name="e_flip")
             for jb in range(N_BLOCKS):
-                nc.tensor.transpose(e_flip[:, jb * P:(jb + 1) * P], e_bf[mb][:, jb * P:(jb + 1) * P], identity[:])
+                nc.tensor.transpose(e_flip[:, jb * P:(jb + 1) * P], e_bf[:, jb * P:(jb + 1) * P], identity[:])
             e_t = work.tile([P, N], BF16, name="e_t")
-            if mb == 0:
-                nc.vector.tensor_copy(e_t[:], e_flip[:])
-            else:
-                nc.scalar.copy(e_t[:], e_flip[:])
+            nc.scalar.copy(e_t[:], e_flip[:])
+
+            o_ps = products.tile([P, D], F32, name="o_ps")
             for jb in range(N_BLOCKS):
-                nc.tensor.matmul(o_ps[mb][:], e_t[:, jb * P:(jb + 1) * P], v_sb[:, jb, :],
+                nc.tensor.matmul(o_ps[:], e_t[:, jb * P:(jb + 1) * P], v_sb[:, jb, :],
                                  start=(jb == 0), stop=(jb == N_BLOCKS - 1))
-
-        z = held.tile([P, M_BLOCKS, N // SPLIT], F32, name="z")
-        for mb in range(M_BLOCKS):
-            e = work.tile([P, N], F32, name="e")
-            nc.scalar.activation(e[:], sc[mb][:], EXP, bias=shift[mb][:], scale=SCALE)
-            nc.vector.reduce_sum(z[:, mb, :], e[:].rearrange("m (t s) -> m t s", s=SPLIT), axis=X)
-        mx = held.tile([P, M_BLOCKS], F32, name="mx")
-        nc.vector.reduce_max(mx[:], z[:], axis=X)
-        inv_mx = held.tile([P, M_BLOCKS], F32, name="inv_mx")
-        nc.vector.reciprocal(inv_mx[:], mx[:])
-
-        o_sb = [work.tile([P, D], F32, name="o_sb") for mb in range(M_BLOCKS)]
-        nc.scalar.mul(o_sb[0][:], o_ps[0][:], inv_mx[:, 0:1])
-        nc.vector.tensor_scalar_mul(o_sb[1][:], o_ps[1][:], inv_mx[:, 1:2])
-        nc.scalar.dma_start(out[0:P, :], o_sb[0][:])
-        nc.sync.dma_start(out[P:2 * P, :], o_sb[1][:])
+            o_sb = work.tile([P, D], F32, name="o_sb")
+            nc.vector.tensor_scalar_mul(o_sb[:], o_ps[:], inv_mx[:])
+            store = nc.sync if mb == 0 else nc.scalar
+            store.dma_start(out[mb * P:(mb + 1) * P, :], o_sb[:])

@@ -43,6 +43,8 @@ def tile_spgqaflashdecodeiris_kernel(tc, k_cache, q, v, offs, out):
 
         identity = held.tile([P, P], BF16, name="identity")
         make_identity(nc, identity[:])
+        identity_f32 = held.tile([P, P], F32, name="identity_f32")
+        make_identity(nc, identity_f32[:])
 
         k_t = held.tile([D, S], BF16, name="k_t")
         for half in range(2):
@@ -65,8 +67,6 @@ def tile_spgqaflashdecodeiris_kernel(tc, k_cache, q, v, offs, out):
             nc.vector.tensor_scalar(scaled[:], sc[mb][:], -SCALE, None, op0=MULT, op1=MIN, accum_out=shift[:])
             e = work.tile([P, N], F32, name="e")
             nc.scalar.activation(e[:], sc[mb][:], EXP, bias=shift[:], scale=SCALE)
-            e_bf = work.tile([P, N], BF16, name="e_bf")
-            nc.vector.tensor_copy(e_bf[:], e[:])
 
             z = work.tile([P, N // SPLIT], F32, name="z")
             nc.vector.reduce_sum(z[:], e[:].rearrange("m (t s) -> m t s", s=SPLIT), axis=X)
@@ -75,9 +75,9 @@ def tile_spgqaflashdecodeiris_kernel(tc, k_cache, q, v, offs, out):
             inv_mx = work.tile([P, 1], F32, name="inv_mx")
             nc.vector.reciprocal(inv_mx[:], mx[:])
 
-            e_flip = flipped.tile([P, N], BF16, name="e_flip")
+            e_flip = flipped.tile([P, N], F32, name="e_flip")
             for jb in range(N_BLOCKS):
-                nc.tensor.transpose(e_flip[:, jb * P:(jb + 1) * P], e_bf[:, jb * P:(jb + 1) * P], identity[:])
+                nc.tensor.transpose(e_flip[:, jb * P:(jb + 1) * P], e[:, jb * P:(jb + 1) * P], identity_f32[:])
             e_t = work.tile([P, N], BF16, name="e_t")
             nc.scalar.copy(e_t[:], e_flip[:])
 

@@ -12,6 +12,8 @@ M, N = 256, 512
 SPLIT = 16
 SCALE = D ** -0.5
 S_BLOCKS, M_BLOCKS, N_BLOCKS = S // P, M // P, N // P
+K_PIECES = 4
+PIECE_BLOCKS = S_BLOCKS // K_PIECES
 FLOPS = 2 * M * N * D + 2 * M * N * D
 
 
@@ -20,16 +22,16 @@ def tile_spgqaflashdecodeiris_kernel(tc, k_cache, q, v, offs, out):
     with (
         tc.tile_pool(name="held", bufs=1) as held,
         tc.tile_pool(name="work", bufs=M_BLOCKS) as work,
-        tc.psum_pool(name="flipped", bufs=2) as flipped,
+        tc.psum_pool(name="flipped", bufs=K_PIECES) as flipped,
         tc.psum_pool(name="scores", bufs=M_BLOCKS) as scores,
         tc.psum_pool(name="products", bufs=M_BLOCKS) as products,
     ):
         k_rows = held.tile([P, S_BLOCKS, D], BF16, name="k_rows")
         k_blocks = k_cache.rearrange("(b p) d -> p b d", p=P)
-        nc.sync.dma_start(k_rows[:, 0:2, :], k_blocks[:, 0:2, :])
-        nc.scalar.dma_start(k_rows[:, 2:4, :], k_blocks[:, 2:4, :])
-        nc.sync.dma_start(k_rows[:, 4:6, :], k_blocks[:, 4:6, :])
-        nc.scalar.dma_start(k_rows[:, 6:8, :], k_blocks[:, 6:8, :])
+        for piece in range(K_PIECES):
+            queue = nc.sync if piece % 2 == 0 else nc.scalar
+            b0 = piece * PIECE_BLOCKS
+            queue.dma_start(k_rows[:, b0:b0 + PIECE_BLOCKS, :], k_blocks[:, b0:b0 + PIECE_BLOCKS, :])
         offsets = held.tile([P, N // 16], U16, name="offsets")
         nc.sync.dma_start(offsets[:], offs)
         q_sb = held.tile([D, M], BF16, name="q_sb")
@@ -47,14 +49,15 @@ def tile_spgqaflashdecodeiris_kernel(tc, k_cache, q, v, offs, out):
         make_identity(nc, identity_f32[:])
 
         k_t = held.tile([D, S], BF16, name="k_t")
-        for half in range(2):
-            k_flip = flipped.tile([D, 4 * P], BF16, name="k_flip")
-            for b in range(4):
-                nc.tensor.transpose(k_flip[:, b * P:(b + 1) * P], k_rows[:, 4 * half + b, :], identity[:])
-            if half == 0:
-                nc.vector.tensor_copy(k_t[:, 0:4 * P], k_flip[:])
+        for piece in range(K_PIECES):
+            k_flip = flipped.tile([D, PIECE_BLOCKS * P], BF16, name="k_flip", tag="flip")
+            for b in range(PIECE_BLOCKS):
+                nc.tensor.transpose(k_flip[:, b * P:(b + 1) * P], k_rows[:, piece * PIECE_BLOCKS + b, :], identity[:])
+            columns = k_t[:, piece * PIECE_BLOCKS * P:(piece + 1) * PIECE_BLOCKS * P]
+            if piece % 2 == 0:
+                nc.scalar.copy(columns, k_flip[:])
             else:
-                nc.scalar.copy(k_t[:, 4 * P:8 * P], k_flip[:])
+                nc.vector.tensor_copy(columns, k_flip[:])
 
         sc = [scores.tile([P, N], F32, name="sc") for mb in range(M_BLOCKS)]
         for mb in range(M_BLOCKS):
@@ -75,11 +78,17 @@ def tile_spgqaflashdecodeiris_kernel(tc, k_cache, q, v, offs, out):
             inv_mx = work.tile([P, 1], F32, name="inv_mx")
             nc.vector.reciprocal(inv_mx[:], mx[:])
 
-            e_flip = flipped.tile([P, N], F32, name="e_flip")
-            for jb in range(N_BLOCKS):
-                nc.tensor.transpose(e_flip[:, jb * P:(jb + 1) * P], e[:, jb * P:(jb + 1) * P], identity_f32[:])
             e_t = work.tile([P, N], BF16, name="e_t")
-            nc.scalar.copy(e_t[:], e_flip[:])
+            for half in range(2):
+                e_flip = flipped.tile([P, N // 2], F32, name="e_flip", tag="flip")
+                for b in range(N_BLOCKS // 2):
+                    jb = half * (N_BLOCKS // 2) + b
+                    nc.tensor.transpose(e_flip[:, b * P:(b + 1) * P], e[:, jb * P:(jb + 1) * P], identity_f32[:])
+                columns = e_t[:, half * (N // 2):(half + 1) * (N // 2)]
+                if half == 0:
+                    nc.vector.tensor_copy(columns, e_flip[:])
+                else:
+                    nc.scalar.copy(columns, e_flip[:])
 
             o_ps = products.tile([P, D], F32, name="o_ps")
             for jb in range(N_BLOCKS):

@@ -35,9 +35,7 @@ def tile_spgqaflashdecodeiris_kernel(tc, k_cache, q, v, offs, out):
         offsets = held.tile([P, N // 16], U16, name="offsets")
         nc.sync.dma_start(offsets[:], offs)
         q_sb = held.tile([D, M], BF16, name="q_sb")
-        nc.sync.dma_start(q_sb[:], q)
-        v_sb = held.tile([P, N_BLOCKS, D], BF16, name="v_sb")
-        nc.scalar.dma_start(v_sb[:], v.rearrange("(b p) f -> p b f", p=P))
+        nc.scalar.dma_start(q_sb[:], q)
 
         warm = held.tile([P, 1], F32, name="warm")
         nc.vector.memset(warm[:], 0.0)
@@ -47,6 +45,9 @@ def tile_spgqaflashdecodeiris_kernel(tc, k_cache, q, v, offs, out):
         make_identity(nc, identity[:])
         identity_f32 = held.tile([P, P], F32, name="identity_f32")
         make_identity(nc, identity_f32[:])
+
+        v_sb = held.tile([P, N_BLOCKS, D], BF16, name="v_sb")
+        nc.gpsimd.dma_start(v_sb[:], v.rearrange("(b p) f -> p b f", p=P))
 
         k_t = held.tile([D, S], BF16, name="k_t")
         for piece in range(K_PIECES):

@@ -65,37 +65,42 @@ def tile_spgqaflashdecodeiris_kernel(tc, k_cache, q, v, offs, out):
             nc.tensor.matmul(sc[mb][:], q_sb[:, mb * P:(mb + 1) * P], k_t[:].indirect(offsets[:]),
                              start=True, stop=True)
 
+
+        shift = [work.tile([P, 1], F32, name="shift") for mb in range(M_BLOCKS)]
         for mb in range(M_BLOCKS):
             scaled = work.tile([P, N], BF16, name="scaled")
-            shift = work.tile([P, 1], F32, name="shift")
-            nc.vector.tensor_scalar(scaled[:], sc[mb][:], -SCALE, None, op0=MULT, op1=MIN, accum_out=shift[:])
-            e = work.tile([P, N], F32, name="e")
-            nc.scalar.activation(e[:], sc[mb][:], EXP, bias=shift[:], scale=SCALE)
+            nc.vector.tensor_scalar(scaled[:], sc[mb][:], -SCALE, None, op0=MULT, op1=MIN, accum_out=shift[mb][:])
+        e = [work.tile([P, N], F32, name="e") for mb in range(M_BLOCKS)]
+        for mb in range(M_BLOCKS):
+            nc.scalar.activation(e[mb][:], sc[mb][:], EXP, bias=shift[mb][:], scale=SCALE)
 
-            z = work.tile([P, N // SPLIT], F32, name="z")
-            nc.vector.reduce_sum(z[:], e[:].rearrange("m (t s) -> m t s", s=SPLIT), axis=X)
-            mx = work.tile([P, 1], F32, name="mx")
-            nc.vector.reduce_max(mx[:], z[:], axis=X)
-            inv_mx = work.tile([P, 1], F32, name="inv_mx")
-            nc.vector.reciprocal(inv_mx[:], mx[:])
-
-            e_t = work.tile([P, N], BF16, name="e_t")
+        e_t = [work.tile([P, N], BF16, name="e_t") for mb in range(M_BLOCKS)]
+        for mb in range(M_BLOCKS):
             for half in range(2):
                 e_flip = flipped.tile([P, N // 2], F32, name="e_flip", tag="flip")
                 for b in range(N_BLOCKS // 2):
                     jb = half * (N_BLOCKS // 2) + b
-                    nc.tensor.transpose(e_flip[:, b * P:(b + 1) * P], e[:, jb * P:(jb + 1) * P], identity_f32[:])
-                columns = e_t[:, half * (N // 2):(half + 1) * (N // 2)]
+                    nc.tensor.transpose(e_flip[:, b * P:(b + 1) * P], e[mb][:, jb * P:(jb + 1) * P], identity_f32[:])
+                columns = e_t[mb][:, half * (N // 2):(half + 1) * (N // 2)]
                 if half == 0:
                     nc.vector.tensor_copy(columns, e_flip[:])
                 else:
                     nc.scalar.copy(columns, e_flip[:])
 
+        inv_mx = [work.tile([P, 1], F32, name="inv_mx") for mb in range(M_BLOCKS)]
+        for mb in range(M_BLOCKS):
+            z = work.tile([P, N // SPLIT], F32, name="z")
+            nc.vector.reduce_sum(z[:], e[mb][:].rearrange("m (t s) -> m t s", s=SPLIT), axis=X)
+            mx = work.tile([P, 1], F32, name="mx")
+            nc.vector.reduce_max(mx[:], z[:], axis=X)
+            nc.vector.reciprocal(inv_mx[mb][:], mx[:])
+
+        for mb in range(M_BLOCKS):
             o_ps = products.tile([P, D], F32, name="o_ps")
             for jb in range(N_BLOCKS):
-                nc.tensor.matmul(o_ps[:], e_t[:, jb * P:(jb + 1) * P], v_sb[:, jb, :],
+                nc.tensor.matmul(o_ps[:], e_t[mb][:, jb * P:(jb + 1) * P], v_sb[:, jb, :],
                                  start=(jb == 0), stop=(jb == N_BLOCKS - 1))
             o_sb = work.tile([P, D], F32, name="o_sb")
-            nc.vector.tensor_scalar_mul(o_sb[:], o_ps[:], inv_mx[:])
+            nc.vector.tensor_scalar_mul(o_sb[:], o_ps[:], inv_mx[mb][:])
             store = nc.sync if mb == 0 else nc.scalar
             store.dma_start(out[mb * P:(mb + 1) * P, :], o_sb[:])

@@ -2,7 +2,7 @@ import concourse.mybir as mybir
 from concourse.masks import make_identity
 
 BF16, F32, U16 = mybir.dt.bfloat16, mybir.dt.float32, mybir.dt.uint16
-EXP = mybir.ActivationFunctionType.Exp
+EXP, COPY = mybir.ActivationFunctionType.Exp, mybir.ActivationFunctionType.Copy
 MULT, MIN = mybir.AluOpType.mult, mybir.AluOpType.min
 X = mybir.AxisListType.X
 
@@ -72,7 +72,9 @@ def tile_spgqaflashdecodeiris_kernel(tc, k_cache, q, v, offs, out):
             nc.vector.tensor_scalar(scaled[:], sc[mb][:], -SCALE, None, op0=MULT, op1=MIN, accum_out=shift[mb][:])
         e = [work.tile([P, N], F32, name="e") for mb in range(M_BLOCKS)]
         for mb in range(M_BLOCKS):
-            nc.scalar.activation(e[mb][:], sc[mb][:], EXP, bias=shift[mb][:], scale=SCALE)
+            for half in range(2):
+                cols = slice(half * (N // 2), (half + 1) * (N // 2))
+                nc.scalar.activation(e[mb][:, cols], sc[mb][:, cols], EXP, bias=shift[mb][:], scale=SCALE)
 
         e_t = [work.tile([P, N], BF16, name="e_t") for mb in range(M_BLOCKS)]
         for mb in range(M_BLOCKS):
@@ -82,18 +84,18 @@ def tile_spgqaflashdecodeiris_kernel(tc, k_cache, q, v, offs, out):
                     jb = half * (N_BLOCKS // 2) + b
                     nc.tensor.transpose(e_flip[:, b * P:(b + 1) * P], e[mb][:, jb * P:(jb + 1) * P], identity_f32[:])
                 columns = e_t[mb][:, half * (N // 2):(half + 1) * (N // 2)]
-                if half == 0:
+                if mb == 0:
                     nc.vector.tensor_copy(columns, e_flip[:])
                 else:
                     nc.scalar.copy(columns, e_flip[:])
 
-        inv_mx = [work.tile([P, 1], F32, name="inv_mx") for mb in range(M_BLOCKS)]
+        z = held.tile([P, M_BLOCKS, N // SPLIT], F32, name="z")
         for mb in range(M_BLOCKS):
-            z = work.tile([P, N // SPLIT], F32, name="z")
-            nc.vector.reduce_sum(z[:], e[mb][:].rearrange("m (t s) -> m t s", s=SPLIT), axis=X)
-            mx = work.tile([P, 1], F32, name="mx")
-            nc.vector.reduce_max(mx[:], z[:], axis=X)
-            nc.vector.reciprocal(inv_mx[mb][:], mx[:])
+            nc.vector.reduce_sum(z[:, mb, :], e[mb][:].rearrange("m (t s) -> m t s", s=SPLIT), axis=X)
+        mx = held.tile([P, M_BLOCKS], F32, name="mx")
+        nc.vector.reduce_max(mx[:], z[:], axis=X)
+        inv_mx = held.tile([P, M_BLOCKS], F32, name="inv_mx")
+        nc.vector.reciprocal(inv_mx[:], mx[:])
 
         for mb in range(M_BLOCKS):
             o_ps = products.tile([P, D], F32, name="o_ps")
@@ -101,6 +103,9 @@ def tile_spgqaflashdecodeiris_kernel(tc, k_cache, q, v, offs, out):
                 nc.tensor.matmul(o_ps[:], e_t[mb][:, jb * P:(jb + 1) * P], v_sb[:, jb, :],
                                  start=(jb == 0), stop=(jb == N_BLOCKS - 1))
             o_sb = work.tile([P, D], F32, name="o_sb")
-            nc.vector.tensor_scalar_mul(o_sb[:], o_ps[:], inv_mx[mb][:])
+            if mb == 0:
+                nc.scalar.activation(o_sb[:], o_ps[:], COPY, scale=inv_mx[:, mb:mb + 1])
+            else:
+                nc.vector.tensor_scalar_mul(o_sb[:], o_ps[:], inv_mx[:, mb:mb + 1])
             store = nc.sync if mb == 0 else nc.scalar
             store.dma_start(out[mb * P:(mb + 1) * P, :], o_sb[:])

@@ -27,11 +27,12 @@ def tile_spgqaflashdecodeiris_kernel(tc, k_cache, q, v, offs, out):
         tc.psum_pool(name="products", bufs=M_BLOCKS) as products,
     ):
         k_rows = held.tile([P, S_BLOCKS, D], BF16, name="k_rows")
-        k_blocks = k_cache.rearrange("(b p) d -> p b d", p=P)
         for piece in range(K_PIECES):
             queue = nc.sync if piece % 2 == 0 else nc.scalar
             b0 = piece * PIECE_BLOCKS
-            queue.dma_start(k_rows[:, b0:b0 + PIECE_BLOCKS, :], k_blocks[:, b0:b0 + PIECE_BLOCKS, :])
+            rows = k_cache[b0 * P:(b0 + PIECE_BLOCKS) * P, :]
+            order = "(p b) d -> p b d" if piece < K_PIECES - 1 else "(b p) d -> p b d"
+            queue.dma_start(k_rows[:, b0:b0 + PIECE_BLOCKS, :], rows.rearrange(order, p=P))
         offsets = held.tile([P, N // 16], U16, name="offsets")
         nc.sync.dma_start(offsets[:], offs)
         q_sb = held.tile([D, M], BF16, name="q_sb")
@@ -51,14 +52,19 @@ def tile_spgqaflashdecodeiris_kernel(tc, k_cache, q, v, offs, out):
 
         k_t = held.tile([D, S], BF16, name="k_t")
         for piece in range(K_PIECES):
-            k_flip = flipped.tile([D, PIECE_BLOCKS * P], BF16, name="k_flip", tag="flip")
+            k_flip = flipped.tile([D, PIECE_BLOCKS, P], BF16, name="k_flip", tag="flip")
             for b in range(PIECE_BLOCKS):
-                nc.tensor.transpose(k_flip[:, b * P:(b + 1) * P], k_rows[:, piece * PIECE_BLOCKS + b, :], identity[:])
+                nc.tensor.transpose(k_flip[:, b, :], k_rows[:, piece * PIECE_BLOCKS + b, :], identity[:])
+            source = k_flip[:].rearrange("d b p -> d p b") if piece < K_PIECES - 1 else k_flip[:]
             columns = k_t[:, piece * PIECE_BLOCKS * P:(piece + 1) * PIECE_BLOCKS * P]
-            if piece % 2 == 0:
-                nc.scalar.copy(columns, k_flip[:])
+            if piece < K_PIECES - 1:
+                columns = columns.rearrange("d (p b) -> d p b", b=PIECE_BLOCKS)
             else:
-                nc.vector.tensor_copy(columns, k_flip[:])
+                columns = columns.rearrange("d (b p) -> d b p", p=P)
+            if piece % 2 == 0:
+                nc.scalar.copy(columns, source)
+            else:
+                nc.vector.tensor_copy(columns, source)
 
         sc = [scores.tile([P, N], F32, name="sc") for mb in range(M_BLOCKS)]
         for mb in range(M_BLOCKS):

@@ -90,7 +90,7 @@ def tile_spgqaflashdecodeiris_kernel(tc, k_cache, q, v, offs, out):
                     jb = half * (N_BLOCKS // 2) + b
                     nc.tensor.transpose(e_flip[:, b * P:(b + 1) * P], e[mb][:, jb * P:(jb + 1) * P], identity_f32[:])
                 columns = e_t[mb][:, half * (N // 2):(half + 1) * (N // 2)]
-                if mb == 0:
+                if mb == 0 and half == 0:
                     nc.vector.tensor_copy(columns, e_flip[:])
                 else:
                     nc.scalar.copy(columns, e_flip[:])

@@ -90,10 +90,7 @@ def tile_spgqaflashdecodeiris_kernel(tc, k_cache, q, v, offs, out):
                     jb = half * (N_BLOCKS // 2) + b
                     nc.tensor.transpose(e_flip[:, b * P:(b + 1) * P], e[mb][:, jb * P:(jb + 1) * P], identity_f32[:])
                 columns = e_t[mb][:, half * (N // 2):(half + 1) * (N // 2)]
-                if mb == 0 and half == 0:
-                    nc.vector.tensor_copy(columns, e_flip[:])
-                else:
-                    nc.scalar.copy(columns, e_flip[:])
+                nc.scalar.copy(columns, e_flip[:])
 
         z = held.tile([P, M_BLOCKS, N // SPLIT], F32, name="z")
         for mb in range(M_BLOCKS):

@@ -93,8 +93,9 @@ def tile_spgqaflashdecodeiris_kernel(tc, k_cache, q, v, offs, out):
                 nc.scalar.copy(columns, e_flip[:])
 
         z = held.tile([P, M_BLOCKS, N // SPLIT], F32, name="z")
-        for mb in range(M_BLOCKS):
-            nc.vector.reduce_sum(z[:, mb, :], e[mb][:].rearrange("m (t s) -> m t s", s=SPLIT), axis=X)
+        for mb, first, last in ((0, 0, N), (1, 0, N // 2), (1, N // 2, N)):
+            splits = slice(first // SPLIT, last // SPLIT)
+            nc.vector.reduce_sum(z[:, mb, splits], e[mb][:, first:last].rearrange("m (t s) -> m t s", s=SPLIT), axis=X)
         mx = held.tile([P, M_BLOCKS], F32, name="mx")
         nc.vector.reduce_max(mx[:], z[:], axis=X)
         inv_mx = held.tile([P, M_BLOCKS], F32, name="inv_mx")

@@ -14,6 +14,7 @@ SCALE = D ** -0.5
 S_BLOCKS, M_BLOCKS, N_BLOCKS = S // P, M // P, N // P
 K_PIECES = 4
 PIECE_BLOCKS = S_BLOCKS // K_PIECES
+PSUM_BANKS = 8
 FLOPS = 2 * M * N * D + 2 * M * N * D
 
 
@@ -22,9 +23,8 @@ def tile_spgqaflashdecodeiris_kernel(tc, k_cache, q, v, offs, out):
     with (
         tc.tile_pool(name="held", bufs=1) as held,
         tc.tile_pool(name="work", bufs=M_BLOCKS) as work,
-        tc.psum_pool(name="flipped", bufs=K_PIECES) as flipped,
         tc.psum_pool(name="scores", bufs=M_BLOCKS) as scores,
-        tc.psum_pool(name="products", bufs=M_BLOCKS) as products,
+        tc.psum_pool(name="banks", bufs=PSUM_BANKS - M_BLOCKS) as banks,
     ):
         k_rows = held.tile([P, S_BLOCKS, D], BF16, name="k_rows")
         for piece in range(K_PIECES):
@@ -51,20 +51,23 @@ def tile_spgqaflashdecodeiris_kernel(tc, k_cache, q, v, offs, out):
         nc.gpsimd.dma_start(v_sb[:], v.rearrange("(b p) f -> p b f", p=P))
 
         k_t = held.tile([D, S], BF16, name="k_t")
-        for piece in range(K_PIECES):
-            k_flip = flipped.tile([D, PIECE_BLOCKS, P], BF16, name="k_flip", tag="flip")
+        for piece in range(K_PIECES - 1):
+            k_flip = banks.tile([D, PIECE_BLOCKS, P], BF16, name="k_flip", tag="bank")
             for b in range(PIECE_BLOCKS):
                 nc.tensor.transpose(k_flip[:, b, :], k_rows[:, piece * PIECE_BLOCKS + b, :], identity[:])
-            source = k_flip[:].rearrange("d b p -> d p b") if piece < K_PIECES - 1 else k_flip[:]
-            columns = k_t[:, piece * PIECE_BLOCKS * P:(piece + 1) * PIECE_BLOCKS * P]
-            if piece < K_PIECES - 1:
-                columns = columns.rearrange("d (p b) -> d p b", b=PIECE_BLOCKS)
-            else:
-                columns = columns.rearrange("d (b p) -> d b p", p=P)
+            columns = k_t[:, piece * PIECE_BLOCKS * P:(piece + 1) * PIECE_BLOCKS * P].rearrange("d (p b) -> d p b", b=PIECE_BLOCKS)
+            in_turn = k_flip[:].rearrange("d b p -> d p b")
             if piece % 2 == 0:
-                nc.scalar.copy(columns, source)
+                nc.scalar.copy(columns, in_turn)
             else:
-                nc.vector.tensor_copy(columns, source)
+                nc.vector.tensor_copy(columns, in_turn)
+        for block in range(S_BLOCKS - PIECE_BLOCKS, S_BLOCKS):
+            k_flip = banks.tile([D, P], BF16, name="k_flip", tag="bank")
+            nc.tensor.transpose(k_flip[:], k_rows[:, block, :], identity[:])
+            if block < S_BLOCKS - 1:
+                nc.scalar.copy(k_t[:, block * P:(block + 1) * P], k_flip[:])
+            else:
+                nc.vector.tensor_copy(k_t[:, block * P:(block + 1) * P], k_flip[:])
 
         sc = [scores.tile([P, N], F32, name="sc") for mb in range(M_BLOCKS)]
         for mb in range(M_BLOCKS):
@@ -85,7 +88,7 @@ def tile_spgqaflashdecodeiris_kernel(tc, k_cache, q, v, offs, out):
         e_t = [work.tile([P, N], BF16, name="e_t") for mb in range(M_BLOCKS)]
         for mb in range(M_BLOCKS):
             for half in range(2):
-                e_flip = flipped.tile([P, N // 2], F32, name="e_flip", tag="flip")
+                e_flip = banks.tile([P, N // 2], F32, name="e_flip", tag="bank")
                 for b in range(N_BLOCKS // 2):
                     jb = half * (N_BLOCKS // 2) + b
                     nc.tensor.transpose(e_flip[:, b * P:(b + 1) * P], e[mb][:, jb * P:(jb + 1) * P], identity_f32[:])
@@ -102,7 +105,7 @@ def tile_spgqaflashdecodeiris_kernel(tc, k_cache, q, v, offs, out):
         nc.vector.reciprocal(inv_mx[:], mx[:])
 
         for mb in range(M_BLOCKS):
-            o_ps = products.tile([P, D], F32, name="o_ps")
+            o_ps = banks.tile([P, D], F32, name="o_ps", tag="bank")
             for jb in range(N_BLOCKS):
                 nc.tensor.matmul(o_ps[:], e_t[mb][:, jb * P:(jb + 1) * P], v_sb[:, jb, :],
                                  start=(jb == 0), stop=(jb == N_BLOCKS - 1))
@@ -111,5 +114,5 @@ def tile_spgqaflashdecodeiris_kernel(tc, k_cache, q, v, offs, out):
                 nc.scalar.activation(o_sb[:], o_ps[:], COPY, scale=inv_mx[:, mb:mb + 1])
             else:
                 nc.vector.tensor_scalar_mul(o_sb[:], o_ps[:], inv_mx[:, mb:mb + 1])
-            store = nc.sync if mb == 0 else nc.scalar
+            store = nc.scalar if mb == 0 else nc.sync
             store.dma_start(out[mb * P:(mb + 1) * P, :], o_sb[:])

import concourse.mybir as mybir
from concourse.masks import make_identity

BF16, F32, U16 = mybir.dt.bfloat16, mybir.dt.float32, mybir.dt.uint16
EXP, COPY = mybir.ActivationFunctionType.Exp, mybir.ActivationFunctionType.Copy
MULT, MIN = mybir.AluOpType.mult, mybir.AluOpType.min
X = mybir.AxisListType.X

P = 128
S, D = 1024, 128
M, N = 256, 512
SPLIT = 16
SCALE = D ** -0.5
S_BLOCKS, M_BLOCKS, N_BLOCKS = S // P, M // P, N // P
K_PIECES = 4
PIECE_BLOCKS = S_BLOCKS // K_PIECES
PSUM_BANKS = 8
FLOPS = 2 * M * N * D + 2 * M * N * D


def tile_spgqaflashdecodeiris_kernel(tc, k_cache, q, v, offs, out):
    nc = tc.nc
    with (
        tc.tile_pool(name="held", bufs=1) as held,
        tc.tile_pool(name="work", bufs=M_BLOCKS) as work,
        tc.psum_pool(name="scores", bufs=M_BLOCKS) as scores,
        tc.psum_pool(name="banks", bufs=PSUM_BANKS - M_BLOCKS) as banks,
    ):
        k_rows = held.tile([P, S_BLOCKS, D], BF16, name="k_rows")
        for piece in range(K_PIECES):
            queue = nc.sync if piece % 2 == 0 else nc.scalar
            b0 = piece * PIECE_BLOCKS
            rows = k_cache[b0 * P:(b0 + PIECE_BLOCKS) * P, :]
            order = "(p b) d -> p b d" if piece < K_PIECES - 1 else "(b p) d -> p b d"
            queue.dma_start(k_rows[:, b0:b0 + PIECE_BLOCKS, :], rows.rearrange(order, p=P))
        offsets = held.tile([P, N // 16], U16, name="offsets")
        nc.sync.dma_start(offsets[:], offs)
        q_sb = held.tile([D, M], BF16, name="q_sb")
        nc.scalar.dma_start(q_sb[:], q)

        warm = held.tile([P, 1], F32, name="warm")
        nc.vector.memset(warm[:], 0.0)
        nc.scalar.activation(warm[:], warm[:], EXP)

        identity = held.tile([P, P], BF16, name="identity")
        make_identity(nc, identity[:])
        identity_f32 = held.tile([P, P], F32, name="identity_f32")
        make_identity(nc, identity_f32[:])

        v_sb = held.tile([P, N_BLOCKS, D], BF16, name="v_sb")
        nc.gpsimd.dma_start(v_sb[:], v.rearrange("(b p) f -> p b f", p=P))

        k_t = held.tile([D, S], BF16, name="k_t")
        for piece in range(K_PIECES - 1):
            k_flip = banks.tile([D, PIECE_BLOCKS, P], BF16, name="k_flip", tag="bank")
            for b in range(PIECE_BLOCKS):
                nc.tensor.transpose(k_flip[:, b, :], k_rows[:, piece * PIECE_BLOCKS + b, :], identity[:])
            columns = k_t[:, piece * PIECE_BLOCKS * P:(piece + 1) * PIECE_BLOCKS * P].rearrange("d (p b) -> d p b", b=PIECE_BLOCKS)
            in_turn = k_flip[:].rearrange("d b p -> d p b")
            if piece % 2 == 0:
                nc.scalar.copy(columns, in_turn)
            else:
                nc.vector.tensor_copy(columns, in_turn)
        for block in range(S_BLOCKS - PIECE_BLOCKS, S_BLOCKS):
            k_flip = banks.tile([D, P], BF16, name="k_flip", tag="bank")
            nc.tensor.transpose(k_flip[:], k_rows[:, block, :], identity[:])
            if block < S_BLOCKS - 1:
                nc.scalar.copy(k_t[:, block * P:(block + 1) * P], k_flip[:])
            else:
                nc.vector.tensor_copy(k_t[:, block * P:(block + 1) * P], k_flip[:])

        sc = [scores.tile([P, N], F32, name="sc") for mb in range(M_BLOCKS)]
        for mb in range(M_BLOCKS):
            nc.tensor.matmul(sc[mb][:], q_sb[:, mb * P:(mb + 1) * P], k_t[:].indirect(offsets[:]),
                             start=True, stop=True)


        shift = [work.tile([P, 1], F32, name="shift") for mb in range(M_BLOCKS)]
        for mb in range(M_BLOCKS):
            scaled = work.tile([P, N], BF16, name="scaled")
            nc.vector.tensor_scalar(scaled[:], sc[mb][:], -SCALE, None, op0=MULT, op1=MIN, accum_out=shift[mb][:])
        e = [work.tile([P, N], F32, name="e") for mb in range(M_BLOCKS)]
        for mb in range(M_BLOCKS):
            for half in range(2):
                cols = slice(half * (N // 2), (half + 1) * (N // 2))
                nc.scalar.activation(e[mb][:, cols], sc[mb][:, cols], EXP, bias=shift[mb][:], scale=SCALE)

        e_t = [work.tile([P, N], BF16, name="e_t") for mb in range(M_BLOCKS)]
        for mb in range(M_BLOCKS):
            for half in range(2):
                e_flip = banks.tile([P, N // 2], F32, name="e_flip", tag="bank")
                for b in range(N_BLOCKS // 2):
                    jb = half * (N_BLOCKS // 2) + b
                    nc.tensor.transpose(e_flip[:, b * P:(b + 1) * P], e[mb][:, jb * P:(jb + 1) * P], identity_f32[:])
                columns = e_t[mb][:, half * (N // 2):(half + 1) * (N // 2)]
                nc.scalar.copy(columns, e_flip[:])

        z = held.tile([P, M_BLOCKS, N // SPLIT], F32, name="z")
        for mb, first, last in ((0, 0, N), (1, 0, N // 2), (1, N // 2, N)):
            splits = slice(first // SPLIT, last // SPLIT)
            nc.vector.reduce_sum(z[:, mb, splits], e[mb][:, first:last].rearrange("m (t s) -> m t s", s=SPLIT), axis=X)
        mx = held.tile([P, M_BLOCKS], F32, name="mx")
        nc.vector.reduce_max(mx[:], z[:], axis=X)
        inv_mx = held.tile([P, M_BLOCKS], F32, name="inv_mx")
        nc.vector.reciprocal(inv_mx[:], mx[:])

        for mb in range(M_BLOCKS):
            o_ps = banks.tile([P, D], F32, name="o_ps", tag="bank")
            for jb in range(N_BLOCKS):
                nc.tensor.matmul(o_ps[:], e_t[mb][:, jb * P:(jb + 1) * P], v_sb[:, jb, :],
                                 start=(jb == 0), stop=(jb == N_BLOCKS - 1))
            o_sb = work.tile([P, D], F32, name="o_sb")
            if mb == 0:
                nc.scalar.activation(o_sb[:], o_ps[:], COPY, scale=inv_mx[:, mb:mb + 1])
            else:
                nc.vector.tensor_scalar_mul(o_sb[:], o_ps[:], inv_mx[:, mb:mb + 1])
            store = nc.scalar if mb == 0 else nc.sync
            store.dma_start(out[mb * P:(mb + 1) * P, :], o_sb[:])
